import numpy as np
import ml_dtypes


def mxq(x, axis, fmt="e4m3"):
    dtype, down = {"e4m3": (ml_dtypes.float8_e4m3fn, 7), "e5m2": (ml_dtypes.float8_e5m2, 14)}[fmt]
    v = np.moveaxis(np.asarray(x, np.float32).astype(ml_dtypes.bfloat16).astype(np.float64), axis, -1)
    blocks = v.reshape(v.shape[:-1] + (-1, 32))
    amax = np.abs(blocks).max(-1, keepdims=True)
    byte = np.maximum(np.where(amax > 0, np.frexp(amax)[1] - 1 + 127, 0) - down, 1)
    scale = np.exp2(byte - 127.0)
    codes = (blocks / scale).astype(np.float32).astype(dtype).astype(np.float64)
    return np.moveaxis((codes * scale).reshape(v.shape), -1, axis)


WIDE = False


def mx_kscale(k):
    if not WIDE:
        return np.ones(k)
    levels = np.array([20, -20, 10, -10, 0])
    a = np.random.permutation(np.resize(levels, k // 512 * 4)).reshape(k // 512, 4)
    idx = np.arange(k)
    return np.exp2(a[idx // 512, idx % 128 // 32])


BF16 = ml_dtypes.bfloat16


def bf(x):
    return np.asarray(x, np.float32).astype(BF16)


def f64(x):
    return np.asarray(x).astype(np.float64)


B, T, HP, WP, NH, D, DFF = 16, 7, 3, 3, 16, 1024, 4096
HW = HP * WP
N = 1 + HW * T


def setup_inputs():
    u = mx_kscale(D)
    c = np.random.standard_normal((B * T, 1 + HW, D)) * 1.5 / np.sqrt(1 + HW)
    c[:, 0, :] *= 5.0
    xr = np.random.standard_normal((B, N, D)) * 1.1
    w = np.random.standard_normal((D, D)) / np.sqrt(D) / u[None, :]
    b = 0.1 * np.random.standard_normal(D)
    g = np.random.standard_normal((B, N, D)) * np.exp2(np.random.randint(-12, 1, (B, N, 1))) * 16.0 * u
    return {"ctx_s": bf(c),
            "x_res": bf(xr),
            "s_out_w": bf(w),
            "s_out_b": bf(b),
            "grad_out": bf(g)}


def reference(ctx_s, x_res, s_out_w, s_out_b, grad_out):
    g2 = f64(grad_out).reshape(B * N, D)
    h = mxq(g2, 1, "e5m2") @ mxq(f64(s_out_w), 1, "e4m3").T
    h = h.reshape(B, N, D)
    cls = np.broadcast_to(h[:, :1, :] / T, (B, T, D)).reshape(B * T, 1, D)
    pat = h[:, 1:, :].reshape(B, HW, T, D).swapaxes(1, 2).reshape(B * T, HW, D)
    return np.concatenate([cls, pat], axis=1)

@@ -1,0 +1,164 @@
+from contextlib import ExitStack
+
+import concourse.mybir as mybir
+from concourse.masks import make_identity
+
+F32 = mybir.dt.float32
+BF16 = mybir.dt.bfloat16
+U32 = mybir.dt.uint32
+U8 = mybir.dt.uint8
+E4M3_X4 = mybir.dt.float8_e4m3fn_x4
+E5M2_X4 = mybir.dt.float8_e5m2_x4
+
+P = 128
+SAMPLES = 16
+FRAMES = 7
+PATCHES = 9
+TOKENS = 64
+D = 1024
+PACK = 4
+PASSES = D // (P * PACK)
+PLANES = 2
+N_HALF = 512
+HALVES = D // N_HALF
+PAIR_ROWS = 2 * P
+PAIR_SAMPLES = PAIR_ROWS // TOKENS
+W_PAIRS = D // PAIR_ROWS
+G_PAIRS = SAMPLES * TOKENS // PAIR_ROWS
+CLASS_COLS = SAMPLES
+
+FLOPS = 2 * SAMPLES * TOKENS * D * D
+BYTES = 2 * (SAMPLES * TOKENS * D + D * D) + 4 * SAMPLES * FRAMES * (1 + PATCHES) * D
+
+
+def transpose_pass(nc, banks, raw, ident, c):
+    words = raw[:].bitcast(F32)
+    bank = banks.tile([P, PLANES, PAIR_ROWS], F32, name="bank")
+    for u in range(PLANES):
+        first = (c * PLANES + u) * P
+        for blk in range(PAIR_ROWS // P):
+            nc.tensor.transpose(
+                out=bank[:, u, blk * P : (blk + 1) * P],
+                in_=words[:, blk, first : first + P],
+                identity=ident[:],
+            )
+    return bank
+
+
+def copy_words(nc, c, out, in_):
+    if c == 0:
+        nc.vector.tensor_copy(out=out, in_=in_)
+    else:
+        nc.scalar.copy(out=out, in_=in_)
+
+
+def tile_timesformerlayer_pc_kernel(tc, ctx_s, x_res, s_out_w, s_out_b, grad_out, out):
+    nc = tc.nc
+    with ExitStack() as ctx:
+        keep = ctx.enter_context(tc.tile_pool(name="keep", bufs=1))
+        results = ctx.enter_context(tc.tile_pool(name="results", bufs=6))
+        banks = ctx.enter_context(tc.psum_pool(name="banks", bufs=4))
+        sums = ctx.enter_context(tc.psum_pool(name="sums", bufs=4))
+
+        w_rows = s_out_w.rearrange("(pair blk p) k -> pair p blk k", blk=2, p=P)
+        g_rows = grad_out.flatten_outer_dims().rearrange("(pair blk p) k -> pair p blk k", blk=2, p=P)
+        w_raw = [keep.tile([P, 2, D], BF16, name="w_raw%d" % pair) for pair in range(W_PAIRS)]
+        g_raw = [keep.tile([P, 2, D], BF16, name="g_raw%d" % pair) for pair in range(G_PAIRS)]
+        for pair in range(W_PAIRS // HALVES):
+            nc.sync.dma_start(out=w_raw[pair][:], in_=w_rows[pair])
+        for pair in range(G_PAIRS):
+            nc.sync.dma_start(out=g_raw[pair][:], in_=g_rows[pair])
+        for pair in range(W_PAIRS // HALVES, W_PAIRS):
+            nc.sync.dma_start(out=w_raw[pair][:], in_=w_rows[pair])
+
+        ident = keep.tile([P, P], F32, name="ident")
+        make_identity(nc, ident[:])
+
+        w_grouped = keep.tile([P, PASSES, D * PACK], BF16, name="w_grouped", align_bytes=64)
+        w_codes = keep.tile([P, PASSES, D], U32, name="w_codes", align_bytes=64)
+        w_scales = keep.tile([P, PASSES, D], U8, name="w_scales", align_bytes=64)
+        w_words = w_grouped[:].bitcast(F32).rearrange("q c (i u) -> q c i u", u=PLANES)
+        g_grouped = keep.tile([P, PATCHES, PASSES * P * PACK], BF16, name="g_grouped", align_bytes=64)
+        g_codes = keep.tile([P, PATCHES, PASSES * P], U32, name="g_codes", align_bytes=64)
+        g_scales = keep.tile([P, PATCHES, PASSES * P], U8, name="g_scales", align_bytes=64)
+        g_words = g_grouped[:].bitcast(F32).rearrange("q p (c m u) -> q p c m u", c=PASSES, u=PLANES)
+
+        spare = g_grouped[:].rearrange("q p (c x) -> q p c x", c=PASSES)[:, 1:, :, : CLASS_COLS * PACK]
+        nc.vector.memset(spare, 0.0)
+
+        def prepare_w(pair):
+            rows = slice(pair * PAIR_ROWS, (pair + 1) * PAIR_ROWS)
+            for c in range(PASSES):
+                bank = transpose_pass(nc, banks, w_raw[pair], ident, c)
+                copy_words(nc, c, w_words[:, c, rows, :], bank[:].rearrange("q u i -> q i u"))
+                nc.vector.quantize_mx(
+                    out=w_codes[:, c, rows].bitcast(E4M3_X4),
+                    scales=w_scales[:, c, rows],
+                    in_=w_grouped[:, c, pair * PAIR_ROWS * PACK : (pair + 1) * PAIR_ROWS * PACK],
+                )
+
+        def prepare_g(pair):
+            first_class = pair * PAIR_SAMPLES
+            first_patch = CLASS_COLS + pair * PAIR_SAMPLES * FRAMES
+            for c in range(PASSES):
+                bank = transpose_pass(nc, banks, g_raw[pair], ident, c)
+                tokens = bank[:].rearrange("q u (b n) -> q u b n", n=TOKENS)
+                copy_words(
+                    nc,
+                    c,
+                    g_words[:, :, c, first_patch : first_patch + PAIR_SAMPLES * FRAMES, :].rearrange(
+                        "q p (b t) u -> q b p t u", t=FRAMES
+                    ),
+                    tokens[:, :, :, 1:].rearrange("q u b (p t) -> q b p t u", t=FRAMES),
+                )
+                copy_words(
+                    nc,
+                    c,
+                    g_words[:, 0, c, first_class : first_class + PAIR_SAMPLES, :],
+                    tokens[:, :, :, 0].rearrange("q u b -> q b u"),
+                )
+
+        def quantise_g(p):
+            nc.vector.quantize_mx(
+                out=g_codes[:, p, :].bitcast(E5M2_X4), scales=g_scales[:, p, :], in_=g_grouped[:, p, :]
+            )
+
+        def multiply(p, half):
+            cols = slice(half * N_HALF, (half + 1) * N_HALF)
+            acc = sums.tile([P, N_HALF], F32, name="acc")
+            for c in range(PASSES):
+                nc.tensor.matmul_mx(
+                    out=acc[:],
+                    lhsT=g_codes[:, p, c * P : (c + 1) * P].bitcast(E5M2_X4),
+                    lhsT_scale=g_scales[:, p, c * P : (c + 1) * P],
+                    rhs=w_codes[:, c, cols].bitcast(E4M3_X4),
+                    rhs_scale=w_scales[:, c, cols],
+                    start=(c == 0),
+                    stop=(c == PASSES - 1),
+                )
+            h_rows = results.tile([P, N_HALF], F32, name="h_rows")
+            if p % 2 == 0:
+                nc.vector.tensor_copy(out=h_rows[:], in_=acc[:])
+                nc.sync.dma_start(out=out[:, 1 + p, cols], in_=h_rows[CLASS_COLS:, :])
+            else:
+                nc.scalar.copy(out=h_rows[:], in_=acc[:])
+                nc.gpsimd.dma_start(out=out[:, 1 + p, cols], in_=h_rows[CLASS_COLS:, :])
+            if p == 0:
+                class_rows = results.tile([CLASS_COLS, N_HALF], F32, name="class_rows")
+                nc.vector.tensor_scalar_mul(out=class_rows[:], in0=acc[:CLASS_COLS, :], scalar1=1.0 / FRAMES)
+                nc.sync.dma_start(
+                    out=out.rearrange("(b t) r d -> b t r d", t=FRAMES)[:, :, 0, cols],
+                    in_=class_rows[:].unsqueeze(1).to_broadcast([SAMPLES, FRAMES, N_HALF]),
+                )
+
+        for pair in range(W_PAIRS // HALVES):
+            prepare_w(pair)
+        for pair in range(G_PAIRS):
+            prepare_g(pair)
+        for p in range(PATCHES):
+            quantise_g(p)
+        for pair in range(W_PAIRS // HALVES, W_PAIRS):
+            prepare_w(pair)
+        for half in range(HALVES):
+            for p in range(PATCHES):
+                multiply(p, half)

@@ -26,6 +26,7 @@ PAIR_SAMPLES = PAIR_ROWS // TOKENS
 W_PAIRS = D // PAIR_ROWS
 G_PAIRS = SAMPLES * TOKENS // PAIR_ROWS
 CLASS_COLS = SAMPLES
+STORE_TILES = 3
 
 FLOPS = 2 * SAMPLES * TOKENS * D * D
 BYTES = 2 * (SAMPLES * TOKENS * D + D * D) + 4 * SAMPLES * FRAMES * (1 + PATCHES) * D
@@ -45,120 +46,103 @@ def transpose_pass(nc, banks, raw, ident, c):
     return bank
 
 
-def copy_words(nc, c, out, in_):
-    if c == 0:
-        nc.vector.tensor_copy(out=out, in_=in_)
-    else:
-        nc.scalar.copy(out=out, in_=in_)
-
-
 def tile_timesformerlayer_pc_kernel(tc, ctx_s, x_res, s_out_w, s_out_b, grad_out, out):
     nc = tc.nc
     with ExitStack() as ctx:
         keep = ctx.enter_context(tc.tile_pool(name="keep", bufs=1))
-        results = ctx.enter_context(tc.tile_pool(name="results", bufs=6))
         banks = ctx.enter_context(tc.psum_pool(name="banks", bufs=4))
         sums = ctx.enter_context(tc.psum_pool(name="sums", bufs=4))
+        ctx.enter_context(tc.manual_schedule())
 
-        w_rows = s_out_w.rearrange("(pair blk p) k -> pair p blk k", blk=2, p=P)
         g_rows = grad_out.flatten_outer_dims().rearrange("(pair blk p) k -> pair p blk k", blk=2, p=P)
-        w_raw = [keep.tile([P, 2, D], BF16, name="w_raw%d" % pair) for pair in range(W_PAIRS)]
+        w_rows = s_out_w.rearrange("(pair blk p) k -> pair p blk k", blk=2, p=P)
         g_raw = [keep.tile([P, 2, D], BF16, name="g_raw%d" % pair) for pair in range(G_PAIRS)]
-        for pair in range(W_PAIRS // HALVES):
-            nc.sync.dma_start(out=w_raw[pair][:], in_=w_rows[pair])
+        w_raw = [keep.tile([P, 2, D], BF16, name="w_raw%d" % pair) for pair in range(W_PAIRS)]
         for pair in range(G_PAIRS):
             nc.sync.dma_start(out=g_raw[pair][:], in_=g_rows[pair])
-        for pair in range(W_PAIRS // HALVES, W_PAIRS):
+        for pair in range(W_PAIRS):
             nc.sync.dma_start(out=w_raw[pair][:], in_=w_rows[pair])
 
         ident = keep.tile([P, P], F32, name="ident")
         make_identity(nc, ident[:])
 
-        w_grouped = keep.tile([P, PASSES, D * PACK], BF16, name="w_grouped", align_bytes=64)
-        w_codes = keep.tile([P, PASSES, D], U32, name="w_codes", align_bytes=64)
-        w_scales = keep.tile([P, PASSES, D], U8, name="w_scales", align_bytes=64)
-        w_words = w_grouped[:].bitcast(F32).rearrange("q c (i u) -> q c i u", u=PLANES)
         g_grouped = keep.tile([P, PATCHES, PASSES * P * PACK], BF16, name="g_grouped", align_bytes=64)
         g_codes = keep.tile([P, PATCHES, PASSES * P], U32, name="g_codes", align_bytes=64)
         g_scales = keep.tile([P, PATCHES, PASSES * P], U8, name="g_scales", align_bytes=64)
         g_words = g_grouped[:].bitcast(F32).rearrange("q p (c m u) -> q p c m u", c=PASSES, u=PLANES)
+        w_grouped = keep.tile([P, PASSES, D * PACK], BF16, name="w_grouped", align_bytes=64)
+        w_codes = keep.tile([P, PASSES, D], U32, name="w_codes", align_bytes=64)
+        w_scales = keep.tile([P, PASSES, D], U8, name="w_scales", align_bytes=64)
+        w_words = w_grouped[:].bitcast(F32).rearrange("q c (i u) -> q c i u", u=PLANES)
 
         spare = g_grouped[:].rearrange("q p (c x) -> q p c x", c=PASSES)[:, 1:, :, : CLASS_COLS * PACK]
         nc.vector.memset(spare, 0.0)
 
-        def prepare_w(pair):
+        for pair in range(G_PAIRS):
+            first_class = pair * PAIR_SAMPLES
+            first_patch = CLASS_COLS + pair * PAIR_SAMPLES * FRAMES
+            for c in range(PASSES):
+                bank = transpose_pass(nc, banks, g_raw[pair], ident, c)
+                tokens = bank[:].rearrange("q u (b n) -> q u b n", n=TOKENS)
+                patch_out = g_words[:, :, c, first_patch : first_patch + PAIR_SAMPLES * FRAMES, :].rearrange(
+                    "q p (b t) u -> q b p t u", t=FRAMES
+                )
+                patch_in = tokens[:, :, :, 1:].rearrange("q u b (p t) -> q b p t u", t=FRAMES)
+                class_out = g_words[:, 0, c, first_class : first_class + PAIR_SAMPLES, :]
+                class_in = tokens[:, :, :, 0].rearrange("q u b -> q b u")
+                if c == 0:
+                    nc.vector.tensor_copy(out=patch_out, in_=patch_in)
+                    nc.vector.tensor_copy(out=class_out, in_=class_in)
+                else:
+                    nc.scalar.copy(out=patch_out, in_=patch_in)
+                    nc.scalar.copy(out=class_out, in_=class_in)
+        for p in range(PATCHES):
+            nc.vector.quantize_mx(
+                out=g_codes[:, p, :].bitcast(E5M2_X4), scales=g_scales[:, p, :], in_=g_grouped[:, p, :]
+            )
+
+        for pair in range(W_PAIRS):
             rows = slice(pair * PAIR_ROWS, (pair + 1) * PAIR_ROWS)
             for c in range(PASSES):
                 bank = transpose_pass(nc, banks, w_raw[pair], ident, c)
-                copy_words(nc, c, w_words[:, c, rows, :], bank[:].rearrange("q u i -> q i u"))
+                nc.scalar.copy(out=w_words[:, c, rows, :], in_=bank[:].rearrange("q u i -> q i u"))
+            for c in range(PASSES):
                 nc.vector.quantize_mx(
                     out=w_codes[:, c, rows].bitcast(E4M3_X4),
                     scales=w_scales[:, c, rows],
                     in_=w_grouped[:, c, pair * PAIR_ROWS * PACK : (pair + 1) * PAIR_ROWS * PACK],
                 )
 
-        def prepare_g(pair):
-            first_class = pair * PAIR_SAMPLES
-            first_patch = CLASS_COLS + pair * PAIR_SAMPLES * FRAMES
-            for c in range(PASSES):
-                bank = transpose_pass(nc, banks, g_raw[pair], ident, c)
-                tokens = bank[:].rearrange("q u (b n) -> q u b n", n=TOKENS)
-                copy_words(
-                    nc,
-                    c,
-                    g_words[:, :, c, first_patch : first_patch + PAIR_SAMPLES * FRAMES, :].rearrange(
-                        "q p (b t) u -> q b p t u", t=FRAMES
-                    ),
-                    tokens[:, :, :, 1:].rearrange("q u b (p t) -> q b p t u", t=FRAMES),
-                )
-                copy_words(
-                    nc,
-                    c,
-                    g_words[:, 0, c, first_class : first_class + PAIR_SAMPLES, :],
-                    tokens[:, :, :, 0].rearrange("q u b -> q b u"),
-                )
-
-        def quantise_g(p):
-            nc.vector.quantize_mx(
-                out=g_codes[:, p, :].bitcast(E5M2_X4), scales=g_scales[:, p, :], in_=g_grouped[:, p, :]
-            )
-
-        def multiply(p, half):
-            cols = slice(half * N_HALF, (half + 1) * N_HALF)
-            acc = sums.tile([P, N_HALF], F32, name="acc")
-            for c in range(PASSES):
-                nc.tensor.matmul_mx(
-                    out=acc[:],
-                    lhsT=g_codes[:, p, c * P : (c + 1) * P].bitcast(E5M2_X4),
-                    lhsT_scale=g_scales[:, p, c * P : (c + 1) * P],
-                    rhs=w_codes[:, c, cols].bitcast(E4M3_X4),
-                    rhs_scale=w_scales[:, c, cols],
-                    start=(c == 0),
-                    stop=(c == PASSES - 1),
-                )
-            h_rows = results.tile([P, N_HALF], F32, name="h_rows")
-            if p % 2 == 0:
-                nc.vector.tensor_copy(out=h_rows[:], in_=acc[:])
-                nc.sync.dma_start(out=out[:, 1 + p, cols], in_=h_rows[CLASS_COLS:, :])
-            else:
-                nc.scalar.copy(out=h_rows[:], in_=acc[:])
-                nc.gpsimd.dma_start(out=out[:, 1 + p, cols], in_=h_rows[CLASS_COLS:, :])
-            if p == 0:
-                class_rows = results.tile([CLASS_COLS, N_HALF], F32, name="class_rows")
-                nc.vector.tensor_scalar_mul(out=class_rows[:], in0=acc[:CLASS_COLS, :], scalar1=1.0 / FRAMES)
-                nc.sync.dma_start(
-                    out=out.rearrange("(b t) r d -> b t r d", t=FRAMES)[:, :, 0, cols],
-                    in_=class_rows[:].unsqueeze(1).to_broadcast([SAMPLES, FRAMES, N_HALF]),
-                )
-
-        for pair in range(W_PAIRS // HALVES):
-            prepare_w(pair)
-        for pair in range(G_PAIRS):
-            prepare_g(pair)
-        for p in range(PATCHES):
-            quantise_g(p)
-        for pair in range(W_PAIRS // HALVES, W_PAIRS):
-            prepare_w(pair)
         for half in range(HALVES):
-            for p in range(PATCHES):
-                multiply(p, half)
+            cols = slice(half * N_HALF, (half + 1) * N_HALF)
+            for first_tile in range(0, PATCHES, STORE_TILES):
+                h_rows = keep.tile([P, STORE_TILES, N_HALF], F32, name="h_rows%d_%d" % (half, first_tile))
+                for s in range(STORE_TILES):
+                    p = first_tile + s
+                    acc = sums.tile([P, N_HALF], F32, name="acc")
+                    for c in range(PASSES):
+                        nc.tensor.matmul_mx(
+                            out=acc[:],
+                            lhsT=g_codes[:, p, c * P : (c + 1) * P].bitcast(E5M2_X4),
+                            lhsT_scale=g_scales[:, p, c * P : (c + 1) * P],
+                            rhs=w_codes[:, c, cols].bitcast(E4M3_X4),
+                            rhs_scale=w_scales[:, c, cols],
+                            start=(c == 0),
+                            stop=(c == PASSES - 1),
+                        )
+                    if p % 2 == 0:
+                        nc.vector.tensor_copy(out=h_rows[:, s, :], in_=acc[:])
+                    else:
+                        nc.scalar.copy(out=h_rows[:, s, :], in_=acc[:])
+                    if p == 0:
+                        class_rows = keep.tile([CLASS_COLS, N_HALF], F32, name="class_rows%d" % half)
+                        nc.vector.tensor_scalar_mul(
+                            out=class_rows[:], in0=acc[:CLASS_COLS, :], scalar1=1.0 / FRAMES
+                        )
+                        nc.sync.dma_start(
+                            out=out.rearrange("(b t) r d -> b t r d", t=FRAMES)[:, :, 0, cols],
+                            in_=class_rows[:].unsqueeze(1).to_broadcast([SAMPLES, FRAMES, N_HALF]),
+                        )
+                nc.sync.dma_start(
+                    out=out[:, 1 + first_tile : 1 + first_tile + STORE_TILES, cols], in_=h_rows[CLASS_COLS:, :, :]
+                )

@@ -113,12 +113,14 @@ def tile_timesformerlayer_pc_kernel(tc, ctx_s, x_res, s_out_w, s_out_b, grad_out
                     in_=w_grouped[:, c, pair * PAIR_ROWS * PACK : (pair + 1) * PAIR_ROWS * PACK],
                 )
 
-        for half in range(HALVES):
-            cols = slice(half * N_HALF, (half + 1) * N_HALF)
-            for first_tile in range(0, PATCHES, STORE_TILES):
-                h_rows = keep.tile([P, STORE_TILES, N_HALF], F32, name="h_rows%d_%d" % (half, first_tile))
-                for s in range(STORE_TILES):
-                    p = first_tile + s
+        for first_tile in range(0, PATCHES, STORE_TILES):
+            h_rows = keep.tile([P, STORE_TILES, D], F32, name="h_rows%d" % first_tile)
+            for s in range(STORE_TILES):
+                p = first_tile + s
+                if p == 0:
+                    class_rows = keep.tile([CLASS_COLS, D], F32, name="class_rows")
+                for half in range(HALVES):
+                    cols = slice(half * N_HALF, (half + 1) * N_HALF)
                     acc = sums.tile([P, N_HALF], F32, name="acc")
                     for c in range(PASSES):
                         nc.tensor.matmul_mx(
@@ -130,19 +132,21 @@ def tile_timesformerlayer_pc_kernel(tc, ctx_s, x_res, s_out_w, s_out_b, grad_out
                             start=(c == 0),
                             stop=(c == PASSES - 1),
                         )
-                    if p % 2 == 0:
-                        nc.vector.tensor_copy(out=h_rows[:, s, :], in_=acc[:])
+                    if half == 0:
+                        nc.vector.tensor_copy(out=h_rows[:, s, cols], in_=acc[:])
+                        if p == 0:
+                            nc.vector.tensor_scalar_mul(
+                                out=class_rows[:, cols], in0=acc[:CLASS_COLS, :], scalar1=1.0 / FRAMES
+                            )
                     else:
-                        nc.scalar.copy(out=h_rows[:, s, :], in_=acc[:])
-                    if p == 0:
-                        class_rows = keep.tile([CLASS_COLS, N_HALF], F32, name="class_rows%d" % half)
-                        nc.vector.tensor_scalar_mul(
-                            out=class_rows[:], in0=acc[:CLASS_COLS, :], scalar1=1.0 / FRAMES
-                        )
-                        nc.sync.dma_start(
-                            out=out.rearrange("(b t) r d -> b t r d", t=FRAMES)[:, :, 0, cols],
-                            in_=class_rows[:].unsqueeze(1).to_broadcast([SAMPLES, FRAMES, N_HALF]),
-                        )
-                nc.sync.dma_start(
-                    out=out[:, 1 + first_tile : 1 + first_tile + STORE_TILES, cols], in_=h_rows[CLASS_COLS:, :, :]
-                )
+                        nc.scalar.copy(out=h_rows[:, s, cols], in_=acc[:])
+                        if p == 0:
+                            nc.scalar.mul(out=class_rows[:, cols], in_=acc[:CLASS_COLS, :], mul=1.0 / FRAMES)
+                if p == 0:
+                    nc.sync.dma_start(
+                        out=out.rearrange("(b t) r d -> b t r d", t=FRAMES)[:, :, 0, :],
+                        in_=class_rows[:].unsqueeze(1).to_broadcast([SAMPLES, FRAMES, D]),
+                    )
+            nc.sync.dma_start(
+                out=out[:, 1 + first_tile : 1 + first_tile + STORE_TILES, :], in_=h_rows[CLASS_COLS:, :, :]
+            )

@@ -65,6 +65,12 @@ def tile_timesformerlayer_pc_kernel(tc, ctx_s, x_res, s_out_w, s_out_b, grad_out
 
         ident = keep.tile([P, P], F32, name="ident")
         make_identity(nc, ident[:])
+        spread = keep.tile([P, P], F32, name="spread")
+        nc.vector.memset(spread[:, :CLASS_COLS], 0.0)
+        nc.vector.tensor_copy(
+            out=spread[:, CLASS_COLS:].rearrange("k (b t) -> k b t", t=FRAMES),
+            in_=ident[:, :SAMPLES].unsqueeze(2).to_broadcast([P, SAMPLES, FRAMES]),
+        )
 
         g_grouped = keep.tile([P, PATCHES, PASSES * P * PACK], BF16, name="g_grouped", align_bytes=64)
         g_codes = keep.tile([P, PATCHES, PASSES * P], U32, name="g_codes", align_bytes=64)
@@ -113,14 +119,12 @@ def tile_timesformerlayer_pc_kernel(tc, ctx_s, x_res, s_out_w, s_out_b, grad_out
                     in_=w_grouped[:, c, pair * PAIR_ROWS * PACK : (pair + 1) * PAIR_ROWS * PACK],
                 )
 
-        for first_tile in range(0, PATCHES, STORE_TILES):
-            h_rows = keep.tile([P, STORE_TILES, D], F32, name="h_rows%d" % first_tile)
-            for s in range(STORE_TILES):
-                p = first_tile + s
-                if p == 0:
-                    class_rows = keep.tile([CLASS_COLS, D], F32, name="class_rows")
-                for half in range(HALVES):
-                    cols = slice(half * N_HALF, (half + 1) * N_HALF)
+        for half in range(HALVES):
+            cols = slice(half * N_HALF, (half + 1) * N_HALF)
+            for first_tile in range(0, PATCHES, STORE_TILES):
+                h_rows = keep.tile([P, STORE_TILES, N_HALF], F32, name="h_rows%d_%d" % (half, first_tile))
+                for s in range(STORE_TILES):
+                    p = first_tile + s
                     acc = sums.tile([P, N_HALF], F32, name="acc")
                     for c in range(PASSES):
                         nc.tensor.matmul_mx(
@@ -132,21 +136,19 @@ def tile_timesformerlayer_pc_kernel(tc, ctx_s, x_res, s_out_w, s_out_b, grad_out
                             start=(c == 0),
                             stop=(c == PASSES - 1),
                         )
-                    if half == 0:
-                        nc.vector.tensor_copy(out=h_rows[:, s, cols], in_=acc[:])
-                        if p == 0:
-                            nc.vector.tensor_scalar_mul(
-                                out=class_rows[:, cols], in0=acc[:CLASS_COLS, :], scalar1=1.0 / FRAMES
-                            )
+                    if p % 2 == 0:
+                        nc.vector.tensor_copy(out=h_rows[:, s, :], in_=acc[:])
                     else:
-                        nc.scalar.copy(out=h_rows[:, s, cols], in_=acc[:])
-                        if p == 0:
-                            nc.scalar.mul(out=class_rows[:, cols], in_=acc[:CLASS_COLS, :], mul=1.0 / FRAMES)
-                if p == 0:
-                    nc.sync.dma_start(
-                        out=out.rearrange("(b t) r d -> b t r d", t=FRAMES)[:, :, 0, :],
-                        in_=class_rows[:].unsqueeze(1).to_broadcast([SAMPLES, FRAMES, D]),
-                    )
-            nc.sync.dma_start(
-                out=out[:, 1 + first_tile : 1 + first_tile + STORE_TILES, :], in_=h_rows[CLASS_COLS:, :, :]
-            )
+                        nc.scalar.copy(out=h_rows[:, s, :], in_=acc[:])
+                    if p == 0:
+                        seventh = keep.tile([P, N_HALF], F32, name="seventh%d" % half)
+                        nc.vector.tensor_scalar_mul(out=seventh[:], in0=acc[:], scalar1=1.0 / FRAMES)
+                nc.sync.dma_start(
+                    out=out[:, 1 + first_tile : 1 + first_tile + STORE_TILES, cols], in_=h_rows[CLASS_COLS:, :, :]
+                )
+                if first_tile == 0:
+                    class_acc = sums.tile([P, N_HALF], F32, name="acc")
+                    nc.tensor.matmul(out=class_acc[:], lhsT=spread[:], rhs=seventh[:], start=True, stop=True)
+                    class_rows = keep.tile([P, N_HALF], F32, name="class_rows%d" % half)
+                    nc.scalar.copy(out=class_rows[:], in_=class_acc[:])
+                    nc.sync.dma_start(out=out[:, 0, cols], in_=class_rows[CLASS_COLS:, :])

@@ -34,7 +34,7 @@ BYTES = 2 * (SAMPLES * TOKENS * D + D * D) + 4 * SAMPLES * FRAMES * (1 + PATCHES
 
 def transpose_pass(nc, banks, raw, ident, c):
     words = raw[:].bitcast(F32)
-    bank = banks.tile([P, PLANES, PAIR_ROWS], F32, name="bank")
+    bank = banks.tile([P, PLANES, PAIR_ROWS], F32, name="bank", tag="bank")
     for u in range(PLANES):
         first = (c * PLANES + u) * P
         for blk in range(PAIR_ROWS // P):
@@ -50,8 +50,7 @@ def tile_timesformerlayer_pc_kernel(tc, ctx_s, x_res, s_out_w, s_out_b, grad_out
     nc = tc.nc
     with ExitStack() as ctx:
         keep = ctx.enter_context(tc.tile_pool(name="keep", bufs=1))
-        banks = ctx.enter_context(tc.psum_pool(name="banks", bufs=4))
-        sums = ctx.enter_context(tc.psum_pool(name="sums", bufs=4))
+        banks = ctx.enter_context(tc.psum_pool(name="banks", bufs=8))
         ctx.enter_context(tc.manual_schedule())
 
         g_rows = grad_out.flatten_outer_dims().rearrange("(pair blk p) k -> pair p blk k", blk=2, p=P)
@@ -125,7 +124,7 @@ def tile_timesformerlayer_pc_kernel(tc, ctx_s, x_res, s_out_w, s_out_b, grad_out
                 h_rows = keep.tile([P, STORE_TILES, N_HALF], F32, name="h_rows%d_%d" % (half, first_tile))
                 for s in range(STORE_TILES):
                     p = first_tile + s
-                    acc = sums.tile([P, N_HALF], F32, name="acc")
+                    acc = banks.tile([P, N_HALF], F32, name="acc", tag="bank")
                     for c in range(PASSES):
                         nc.tensor.matmul_mx(
                             out=acc[:],
@@ -146,8 +145,8 @@ def tile_timesformerlayer_pc_kernel(tc, ctx_s, x_res, s_out_w, s_out_b, grad_out
                 nc.sync.dma_start(
                     out=out[:, 1 + first_tile : 1 + first_tile + STORE_TILES, cols], in_=h_rows[CLASS_COLS:, :, :]
                 )
-                if first_tile == 0:
-                    class_acc = sums.tile([P, N_HALF], F32, name="acc")
+                if first_tile == STORE_TILES:
+                    class_acc = banks.tile([P, N_HALF], F32, name="acc", tag="bank")
                     nc.tensor.matmul(out=class_acc[:], lhsT=spread[:], rhs=seventh[:], start=True, stop=True)
                     class_rows = keep.tile([P, N_HALF], F32, name="class_rows%d" % half)
                     nc.scalar.copy(out=class_rows[:], in_=class_acc[:])

@@ -26,7 +26,9 @@ PAIR_SAMPLES = PAIR_ROWS // TOKENS
 W_PAIRS = D // PAIR_ROWS
 G_PAIRS = SAMPLES * TOKENS // PAIR_ROWS
 CLASS_COLS = SAMPLES
-STORE_TILES = 3
+W_HALF_PAIRS = W_PAIRS // HALVES
+LATE_TILE = 3
+SPREAD_TILE = 5
 
 FLOPS = 2 * SAMPLES * TOKENS * D * D
 BYTES = 2 * (SAMPLES * TOKENS * D + D * D) + 4 * SAMPLES * FRAMES * (1 + PATCHES) * D
@@ -53,13 +55,15 @@ def tile_timesformerlayer_pc_kernel(tc, ctx_s, x_res, s_out_w, s_out_b, grad_out
         banks = ctx.enter_context(tc.psum_pool(name="banks", bufs=8))
         ctx.enter_context(tc.manual_schedule())
 
-        g_rows = grad_out.flatten_outer_dims().rearrange("(pair blk p) k -> pair p blk k", blk=2, p=P)
         w_rows = s_out_w.rearrange("(pair blk p) k -> pair p blk k", blk=2, p=P)
-        g_raw = [keep.tile([P, 2, D], BF16, name="g_raw%d" % pair) for pair in range(G_PAIRS)]
+        g_rows = grad_out.flatten_outer_dims().rearrange("(pair blk p) k -> pair p blk k", blk=2, p=P)
         w_raw = [keep.tile([P, 2, D], BF16, name="w_raw%d" % pair) for pair in range(W_PAIRS)]
+        g_raw = [keep.tile([P, 2, D], BF16, name="g_raw%d" % pair) for pair in range(G_PAIRS)]
+        for pair in range(W_HALF_PAIRS):
+            nc.sync.dma_start(out=w_raw[pair][:], in_=w_rows[pair])
         for pair in range(G_PAIRS):
             nc.sync.dma_start(out=g_raw[pair][:], in_=g_rows[pair])
-        for pair in range(W_PAIRS):
+        for pair in range(W_HALF_PAIRS, W_PAIRS):
             nc.sync.dma_start(out=w_raw[pair][:], in_=w_rows[pair])
 
         ident = keep.tile([P, P], F32, name="ident")
@@ -83,34 +87,11 @@ def tile_timesformerlayer_pc_kernel(tc, ctx_s, x_res, s_out_w, s_out_b, grad_out
         spare = g_grouped[:].rearrange("q p (c x) -> q p c x", c=PASSES)[:, 1:, :, : CLASS_COLS * PACK]
         nc.vector.memset(spare, 0.0)
 
-        for pair in range(G_PAIRS):
-            first_class = pair * PAIR_SAMPLES
-            first_patch = CLASS_COLS + pair * PAIR_SAMPLES * FRAMES
-            for c in range(PASSES):
-                bank = transpose_pass(nc, banks, g_raw[pair], ident, c)
-                tokens = bank[:].rearrange("q u (b n) -> q u b n", n=TOKENS)
-                patch_out = g_words[:, :, c, first_patch : first_patch + PAIR_SAMPLES * FRAMES, :].rearrange(
-                    "q p (b t) u -> q b p t u", t=FRAMES
-                )
-                patch_in = tokens[:, :, :, 1:].rearrange("q u b (p t) -> q b p t u", t=FRAMES)
-                class_out = g_words[:, 0, c, first_class : first_class + PAIR_SAMPLES, :]
-                class_in = tokens[:, :, :, 0].rearrange("q u b -> q b u")
-                if c == 0:
-                    nc.vector.tensor_copy(out=patch_out, in_=patch_in)
-                    nc.vector.tensor_copy(out=class_out, in_=class_in)
-                else:
-                    nc.scalar.copy(out=patch_out, in_=patch_in)
-                    nc.scalar.copy(out=class_out, in_=class_in)
-        for p in range(PATCHES):
-            nc.vector.quantize_mx(
-                out=g_codes[:, p, :].bitcast(E5M2_X4), scales=g_scales[:, p, :], in_=g_grouped[:, p, :]
-            )
-
-        for pair in range(W_PAIRS):
+        def prepare_w(pair, copy):
             rows = slice(pair * PAIR_ROWS, (pair + 1) * PAIR_ROWS)
             for c in range(PASSES):
                 bank = transpose_pass(nc, banks, w_raw[pair], ident, c)
-                nc.scalar.copy(out=w_words[:, c, rows, :], in_=bank[:].rearrange("q u i -> q i u"))
+                copy(out=w_words[:, c, rows, :], in_=bank[:].rearrange("q u i -> q i u"))
             for c in range(PASSES):
                 nc.vector.quantize_mx(
                     out=w_codes[:, c, rows].bitcast(E4M3_X4),
@@ -118,36 +99,75 @@ def tile_timesformerlayer_pc_kernel(tc, ctx_s, x_res, s_out_w, s_out_b, grad_out
                     in_=w_grouped[:, c, pair * PAIR_ROWS * PACK : (pair + 1) * PAIR_ROWS * PACK],
                 )
 
-        for half in range(HALVES):
-            cols = slice(half * N_HALF, (half + 1) * N_HALF)
-            for first_tile in range(0, PATCHES, STORE_TILES):
-                h_rows = keep.tile([P, STORE_TILES, N_HALF], F32, name="h_rows%d_%d" % (half, first_tile))
-                for s in range(STORE_TILES):
-                    p = first_tile + s
-                    acc = banks.tile([P, N_HALF], F32, name="acc", tag="bank")
-                    for c in range(PASSES):
-                        nc.tensor.matmul_mx(
-                            out=acc[:],
-                            lhsT=g_codes[:, p, c * P : (c + 1) * P].bitcast(E5M2_X4),
-                            lhsT_scale=g_scales[:, p, c * P : (c + 1) * P],
-                            rhs=w_codes[:, c, cols].bitcast(E4M3_X4),
-                            rhs_scale=w_scales[:, c, cols],
-                            start=(c == 0),
-                            stop=(c == PASSES - 1),
-                        )
-                    if p % 2 == 0:
-                        nc.vector.tensor_copy(out=h_rows[:, s, :], in_=acc[:])
-                    else:
-                        nc.scalar.copy(out=h_rows[:, s, :], in_=acc[:])
-                    if p == 0:
-                        seventh = keep.tile([P, N_HALF], F32, name="seventh%d" % half)
-                        nc.vector.tensor_scalar_mul(out=seventh[:], in0=acc[:], scalar1=1.0 / FRAMES)
-                nc.sync.dma_start(
-                    out=out[:, 1 + first_tile : 1 + first_tile + STORE_TILES, cols], in_=h_rows[CLASS_COLS:, :, :]
+        def prepare_g(pair):
+            first_class = pair * PAIR_SAMPLES
+            first_patch = CLASS_COLS + pair * PAIR_SAMPLES * FRAMES
+            for c in range(PASSES):
+                bank = transpose_pass(nc, banks, g_raw[pair], ident, c)
+                tokens = bank[:].rearrange("q u (b n) -> q u b n", n=TOKENS)
+                copy = nc.vector.tensor_copy if c == 0 else nc.scalar.copy
+                copy(
+                    out=g_words[:, :, c, first_patch : first_patch + PAIR_SAMPLES * FRAMES, :].rearrange(
+                        "q p (b t) u -> q b p t u", t=FRAMES
+                    ),
+                    in_=tokens[:, :, :, 1:].rearrange("q u b (p t) -> q b p t u", t=FRAMES),
                 )
-                if first_tile == STORE_TILES:
-                    class_acc = banks.tile([P, N_HALF], F32, name="acc", tag="bank")
-                    nc.tensor.matmul(out=class_acc[:], lhsT=spread[:], rhs=seventh[:], start=True, stop=True)
-                    class_rows = keep.tile([P, N_HALF], F32, name="class_rows%d" % half)
-                    nc.scalar.copy(out=class_rows[:], in_=class_acc[:])
-                    nc.sync.dma_start(out=out[:, 0, cols], in_=class_rows[CLASS_COLS:, :])
+                copy(
+                    out=g_words[:, 0, c, first_class : first_class + PAIR_SAMPLES, :],
+                    in_=tokens[:, :, :, 0].rearrange("q u b -> q b u"),
+                )
+
+        def store_row(row, half, h_row):
+            nc.sync.dma_start(
+                out=out[:, row, half * N_HALF : (half + 1) * N_HALF], in_=h_row[CLASS_COLS:, :]
+            )
+
+        sevenths = [keep.tile([P, N_HALF], F32, name="seventh%d" % half) for half in range(HALVES)]
+
+        def multiply(p, half):
+            cols = slice(half * N_HALF, (half + 1) * N_HALF)
+            acc = banks.tile([P, N_HALF], F32, name="acc", tag="bank")
+            for c in range(PASSES):
+                nc.tensor.matmul_mx(
+                    out=acc[:],
+                    lhsT=g_codes[:, p, c * P : (c + 1) * P].bitcast(E5M2_X4),
+                    lhsT_scale=g_scales[:, p, c * P : (c + 1) * P],
+                    rhs=w_codes[:, c, cols].bitcast(E4M3_X4),
+                    rhs_scale=w_scales[:, c, cols],
+                    start=(c == 0),
+                    stop=(c == PASSES - 1),
+                )
+            h_row = keep.tile([P, N_HALF], F32, name="h_row%d_%d" % (half, p))
+            if half == 1 and p % 2 == 0:
+                nc.vector.tensor_copy(out=h_row[:], in_=acc[:])
+                if p == 0:
+                    nc.vector.tensor_scalar_mul(out=sevenths[half][:], in0=acc[:], scalar1=1.0 / FRAMES)
+            else:
+                nc.scalar.copy(out=h_row[:], in_=acc[:])
+                if p == 0:
+                    nc.scalar.mul(out=sevenths[half][:], in_=acc[:], mul=1.0 / FRAMES)
+            store_row(1 + p, half, h_row)
+
+        def spread_class_rows(half):
+            class_acc = banks.tile([P, N_HALF], F32, name="class_acc", tag="bank")
+            nc.tensor.matmul(out=class_acc[:], lhsT=spread[:], rhs=sevenths[half][:], start=True, stop=True)
+            class_row = keep.tile([P, N_HALF], F32, name="class_row%d" % half)
+            nc.scalar.copy(out=class_row[:], in_=class_acc[:])
+            store_row(0, half, class_row)
+
+        for pair in range(W_HALF_PAIRS):
+            prepare_w(pair, nc.scalar.copy)
+        for pair in range(G_PAIRS):
+            prepare_g(pair)
+        for p in range(PATCHES):
+            nc.vector.quantize_mx(
+                out=g_codes[:, p, :].bitcast(E5M2_X4), scales=g_scales[:, p, :], in_=g_grouped[:, p, :]
+            )
+        for half in range(HALVES):
+            for p in range(PATCHES):
+                if half == 0 and p == LATE_TILE:
+                    for pair in range(W_HALF_PAIRS, W_PAIRS):
+                        prepare_w(pair, nc.vector.tensor_copy)
+                multiply(p, half)
+                if p == SPREAD_TILE:
+                    spread_class_rows(half)

@@ -25,10 +25,18 @@ PAIR_ROWS = 2 * P
 PAIR_SAMPLES = PAIR_ROWS // TOKENS
 W_PAIRS = D // PAIR_ROWS
 G_PAIRS = SAMPLES * TOKENS // PAIR_ROWS
-CLASS_COLS = SAMPLES
-W_HALF_PAIRS = W_PAIRS // HALVES
-LATE_TILE = 3
-SPREAD_TILE = 5
+
+KINDS = 2
+ROWS = 1 + PATCHES
+LIST_ROWS = ROWS // KINDS
+LIST = SAMPLES * FRAMES * LIST_ROWS
+FULL = LIST // P
+REST = LIST - FULL * P
+REST_COLS = P // KINDS
+LIST_COLS = FULL * P + REST_COLS
+CLASS_STEP = FRAMES * LIST_ROWS
+TILES = [(kind, i) for i in range(FULL) for kind in range(KINDS)]
+LAST = KINDS * FULL
 
 FLOPS = 2 * SAMPLES * TOKENS * D * D
 BYTES = 2 * (SAMPLES * TOKENS * D + D * D) + 4 * SAMPLES * FRAMES * (1 + PATCHES) * D
@@ -48,6 +56,11 @@ def transpose_pass(nc, banks, raw, ident, c):
     return bank
 
 
+def first_class(i):
+    sample = -(-i * P // CLASS_STEP)
+    return sample * CLASS_STEP - i * P, sample
+
+
 def tile_timesformerlayer_pc_kernel(tc, ctx_s, x_res, s_out_w, s_out_b, grad_out, out):
     nc = tc.nc
     with ExitStack() as ctx:
@@ -59,39 +72,60 @@ def tile_timesformerlayer_pc_kernel(tc, ctx_s, x_res, s_out_w, s_out_b, grad_out
         g_rows = grad_out.flatten_outer_dims().rearrange("(pair blk p) k -> pair p blk k", blk=2, p=P)
         w_raw = [keep.tile([P, 2, D], BF16, name="w_raw%d" % pair) for pair in range(W_PAIRS)]
         g_raw = [keep.tile([P, 2, D], BF16, name="g_raw%d" % pair) for pair in range(G_PAIRS)]
-        for pair in range(W_HALF_PAIRS):
+
+        def load_w(pair):
             nc.sync.dma_start(out=w_raw[pair][:], in_=w_rows[pair])
-        for pair in range(G_PAIRS):
+
+        def load_g(pair):
             nc.sync.dma_start(out=g_raw[pair][:], in_=g_rows[pair])
-        for pair in range(W_HALF_PAIRS, W_PAIRS):
-            nc.sync.dma_start(out=w_raw[pair][:], in_=w_rows[pair])
+
+        load_w(0)
+        load_w(1)
+        load_g(0)
+        load_w(2)
+        load_w(3)
+        load_g(1)
+        load_g(2)
+        load_g(3)
 
         ident = keep.tile([P, P], F32, name="ident")
         make_identity(nc, ident[:])
-        spread = keep.tile([P, P], F32, name="spread")
-        nc.vector.memset(spread[:, :CLASS_COLS], 0.0)
-        nc.vector.tensor_copy(
-            out=spread[:, CLASS_COLS:].rearrange("k (b t) -> k b t", t=FRAMES),
-            in_=ident[:, :SAMPLES].unsqueeze(2).to_broadcast([P, SAMPLES, FRAMES]),
-        )
 
-        g_grouped = keep.tile([P, PATCHES, PASSES * P * PACK], BF16, name="g_grouped", align_bytes=64)
-        g_codes = keep.tile([P, PATCHES, PASSES * P], U32, name="g_codes", align_bytes=64)
-        g_scales = keep.tile([P, PATCHES, PASSES * P], U8, name="g_scales", align_bytes=64)
-        g_words = g_grouped[:].bitcast(F32).rearrange("q p (c m u) -> q p c m u", c=PASSES, u=PLANES)
+        g_grouped = keep.tile([P, PASSES, KINDS, LIST_COLS * PACK], BF16, name="g_grouped", align_bytes=64)
+        g_codes = keep.tile([P, LAST + 1, PASSES * P], U32, name="g_codes", align_bytes=64)
+        g_scales = keep.tile([P, LAST + 1, PASSES * P], U8, name="g_scales", align_bytes=64)
+        g_words = g_grouped[:].bitcast(F32).rearrange("q c l (m u) -> q c l m u", u=PLANES)
         w_grouped = keep.tile([P, PASSES, D * PACK], BF16, name="w_grouped", align_bytes=64)
         w_codes = keep.tile([P, PASSES, D], U32, name="w_codes", align_bytes=64)
         w_scales = keep.tile([P, PASSES, D], U8, name="w_scales", align_bytes=64)
         w_words = w_grouped[:].bitcast(F32).rearrange("q c (i u) -> q c i u", u=PLANES)
 
-        spare = g_grouped[:].rearrange("q p (c x) -> q p c x", c=PASSES)[:, 1:, :, : CLASS_COLS * PACK]
-        nc.vector.memset(spare, 0.0)
+        for c in range(PASSES):
+            nc.vector.memset(g_words[:, c, 0], 0.0)
+        nc.vector.memset(g_words[:, :, 1, LIST:], 0.0)
 
-        def prepare_w(pair, copy):
+        is_class = keep.tile([P, FULL + 1], F32, name="is_class")
+        for i in range(FULL + 1):
+            columns = ident[:, first_class(i)[0] : P if i < FULL else REST : CLASS_STEP]
+            nc.vector.reduce_sum(out=is_class[:, i : i + 1], in_=columns, axis=mybir.AxisListType.X)
+        row_scale = keep.tile([P, FULL + 1], F32, name="row_scale")
+        nc.vector.tensor_scalar(
+            out=row_scale[:],
+            in0=is_class[:],
+            scalar1=1.0 / FRAMES - 1.0,
+            scalar2=1.0,
+            op0=mybir.AluOpType.mult,
+            op1=mybir.AluOpType.add,
+        )
+
+        def prepare_w(pair):
             rows = slice(pair * PAIR_ROWS, (pair + 1) * PAIR_ROWS)
             for c in range(PASSES):
                 bank = transpose_pass(nc, banks, w_raw[pair], ident, c)
-                copy(out=w_words[:, c, rows, :], in_=bank[:].rearrange("q u i -> q i u"))
+                nc.scalar.copy(out=w_words[:, c, rows, :], in_=bank[:].rearrange("q u i -> q i u"))
+
+        def quantise_w(pair):
+            rows = slice(pair * PAIR_ROWS, (pair + 1) * PAIR_ROWS)
             for c in range(PASSES):
                 nc.vector.quantize_mx(
                     out=w_codes[:, c, rows].bitcast(E4M3_X4),
@@ -100,74 +134,131 @@ def tile_timesformerlayer_pc_kernel(tc, ctx_s, x_res, s_out_w, s_out_b, grad_out
                 )
 
         def prepare_g(pair):
-            first_class = pair * PAIR_SAMPLES
-            first_patch = CLASS_COLS + pair * PAIR_SAMPLES * FRAMES
+            samples = slice(pair * PAIR_SAMPLES, (pair + 1) * PAIR_SAMPLES)
             for c in range(PASSES):
                 bank = transpose_pass(nc, banks, g_raw[pair], ident, c)
                 tokens = bank[:].rearrange("q u (b n) -> q u b n", n=TOKENS)
+                patches = tokens[:, :, :, 1:].rearrange("q u b (p t) -> q u b p t", t=FRAMES)
                 copy = nc.vector.tensor_copy if c == 0 else nc.scalar.copy
-                copy(
-                    out=g_words[:, :, c, first_patch : first_patch + PAIR_SAMPLES * FRAMES, :].rearrange(
-                        "q p (b t) u -> q b p t u", t=FRAMES
-                    ),
-                    in_=tokens[:, :, :, 1:].rearrange("q u b (p t) -> q b p t u", t=FRAMES),
-                )
-                copy(
-                    out=g_words[:, 0, c, first_class : first_class + PAIR_SAMPLES, :],
-                    in_=tokens[:, :, :, 0].rearrange("q u b -> q b u"),
-                )
+                even, odd = [
+                    g_words[:, c, kind, :LIST].rearrange("q (b t j) u -> q b t j u", t=FRAMES, j=LIST_ROWS)
+                    for kind in range(KINDS)
+                ]
+                copy(out=even[:, samples, 0, 0, :], in_=tokens[:, :, :, 0].rearrange("q u b -> q b u"))
+                copy(out=even[:, samples, :, 1:, :], in_=patches[:, :, :, 1::2, :].rearrange("q u b j t -> q b t j u"))
+                copy(out=odd[:, samples], in_=patches[:, :, :, 0::2, :].rearrange("q u b j t -> q b t j u"))
 
-        def store_row(row, half, h_row):
-            nc.sync.dma_start(
-                out=out[:, row, half * N_HALF : (half + 1) * N_HALF], in_=h_row[CLASS_COLS:, :]
-            )
+        def quantise_g(tile):
+            for c in range(PASSES):
+                if tile < LAST:
+                    pieces = [(TILES[tile][0], TILES[tile][1] * P, P, 0)]
+                else:
+                    pieces = [(kind, FULL * P, REST_COLS, kind * REST_COLS) for kind in range(KINDS)]
+                for kind, source, width, offset in pieces:
+                    columns = slice(c * P + offset, c * P + offset + width)
+                    nc.vector.quantize_mx(
+                        out=g_codes[:, tile, columns].bitcast(E5M2_X4),
+                        scales=g_scales[:, tile, columns],
+                        in_=g_grouped[:, c, kind, source * PACK : (source + width) * PACK],
+                    )
 
-        sevenths = [keep.tile([P, N_HALF], F32, name="seventh%d" % half) for half in range(HALVES)]
+        h_rows = [keep.tile([P, D], F32, name="h_rows%d" % tile) for tile in range(LAST + 1)]
 
-        def multiply(p, half):
+        def multiply(tile, half):
             cols = slice(half * N_HALF, (half + 1) * N_HALF)
             acc = banks.tile([P, N_HALF], F32, name="acc", tag="bank")
             for c in range(PASSES):
                 nc.tensor.matmul_mx(
                     out=acc[:],
-                    lhsT=g_codes[:, p, c * P : (c + 1) * P].bitcast(E5M2_X4),
-                    lhsT_scale=g_scales[:, p, c * P : (c + 1) * P],
+                    lhsT=g_codes[:, tile, c * P : (c + 1) * P].bitcast(E5M2_X4),
+                    lhsT_scale=g_scales[:, tile, c * P : (c + 1) * P],
                     rhs=w_codes[:, c, cols].bitcast(E4M3_X4),
                     rhs_scale=w_scales[:, c, cols],
                     start=(c == 0),
                     stop=(c == PASSES - 1),
                 )
-            h_row = keep.tile([P, N_HALF], F32, name="h_row%d_%d" % (half, p))
-            if half == 1 and p % 2 == 0:
-                nc.vector.tensor_copy(out=h_row[:], in_=acc[:])
-                if p == 0:
-                    nc.vector.tensor_scalar_mul(out=sevenths[half][:], in0=acc[:], scalar1=1.0 / FRAMES)
+            return acc
+
+        def take_out(tile, half, acc):
+            target = h_rows[tile][:, half * N_HALF : (half + 1) * N_HALF]
+            if tile == LAST or TILES[tile][0] == 0:
+                i = FULL if tile == LAST else TILES[tile][1]
+                scale = row_scale[:, i : i + 1]
+                if half == 0:
+                    nc.scalar.activation(
+                        out=target, in_=acc[:], func=mybir.ActivationFunctionType.Copy, scale=scale
+                    )
+                else:
+                    nc.vector.tensor_scalar_mul(out=target, in0=acc[:], scalar1=scale)
+            elif half == 0:
+                nc.scalar.copy(out=target, in_=acc[:])
             else:
-                nc.scalar.copy(out=h_row[:], in_=acc[:])
-                if p == 0:
-                    nc.scalar.mul(out=sevenths[half][:], in_=acc[:], mul=1.0 / FRAMES)
-            store_row(1 + p, half, h_row)
+                nc.vector.tensor_copy(out=target, in_=acc[:])
 
-        def spread_class_rows(half):
-            class_acc = banks.tile([P, N_HALF], F32, name="class_acc", tag="bank")
-            nc.tensor.matmul(out=class_acc[:], lhsT=spread[:], rhs=sevenths[half][:], start=True, stop=True)
-            class_row = keep.tile([P, N_HALF], F32, name="class_row%d" % half)
-            nc.scalar.copy(out=class_row[:], in_=class_acc[:])
-            store_row(0, half, class_row)
+        list_rows = out.rearrange("s r d -> (s r) d").rearrange("(n kind) d -> kind n d", kind=KINDS)
+        class_rows = out.rearrange("(b t) r d -> b t r d", t=FRAMES)
 
-        for pair in range(W_HALF_PAIRS):
-            prepare_w(pair, nc.scalar.copy)
-        for pair in range(G_PAIRS):
-            prepare_g(pair)
-        for p in range(PATCHES):
-            nc.vector.quantize_mx(
-                out=g_codes[:, p, :].bitcast(E5M2_X4), scales=g_scales[:, p, :], in_=g_grouped[:, p, :]
+        def store(tile):
+            if tile < LAST:
+                kind, i = TILES[tile]
+                nc.sync.dma_start(out=list_rows[kind, i * P : (i + 1) * P, :], in_=h_rows[tile][:])
+                return
+            for kind in range(KINDS):
+                first = kind * REST_COLS
+                nc.sync.dma_start(
+                    out=list_rows[kind, FULL * P : LIST, :], in_=h_rows[LAST][first : first + REST, :]
+                )
+
+        def copy_class_rows(i):
+            partition, sample = first_class(i)
+            stop = first_class(i + 1)[1] if i < FULL else SAMPLES
+            rows = h_rows[LAST if i == FULL else TILES.index((0, i))]
+            count = stop - sample
+            source = rows[partition : partition + (count - 1) * CLASS_STEP + 1 : CLASS_STEP, :]
+            nc.gpsimd.dma_start(
+                out=class_rows[sample:stop, 1:, 0, :],
+                in_=source.unsqueeze(1).to_broadcast([count, FRAMES - 1, D]),
             )
-        for half in range(HALVES):
-            for p in range(PATCHES):
-                if half == 0 and p == LATE_TILE:
-                    for pair in range(W_HALF_PAIRS, W_PAIRS):
-                        prepare_w(pair, nc.vector.tensor_copy)
-                multiply(p, half)
-                if p == SPREAD_TILE:
-                    spread_class_rows(half)
+
+        def whole_tile(tile):
+            for half in range(HALVES):
+                take_out(tile, half, multiply(tile, half))
+            store(tile)
+
+        prepare_w(0)
+        prepare_w(1)
+        quantise_w(0)
+        quantise_w(1)
+        prepare_g(0)
+        quantise_g(0)
+        quantise_g(1)
+        prepare_w(2)
+        for tile in (0, 1):
+            take_out(tile, 0, multiply(tile, 0))
+        prepare_w(3)
+        quantise_w(2)
+        quantise_w(3)
+        prepare_g(1)
+        for tile in (0, 1):
+            take_out(tile, 1, multiply(tile, 1))
+            store(tile)
+        quantise_g(2)
+        prepare_g(2)
+        whole_tile(2)
+        quantise_g(4)
+        copy_class_rows(0)
+        prepare_g(3)
+        whole_tile(4)
+        copy_class_rows(1)
+        quantise_g(6)
+        quantise_g(LAST)
+        whole_tile(6)
+        copy_class_rows(2)
+        quantise_g(3)
+        quantise_g(5)
+        whole_tile(LAST)
+        copy_class_rows(3)
+        copy_class_rows(4)
+        quantise_g(7)
+        for tile in (3, 5, 7):
+            whole_tile(tile)

@@ -34,8 +34,9 @@ FULL = LIST // P
 REST = LIST - FULL * P
 REST_COLS = P // KINDS
 LIST_COLS = FULL * P + REST_COLS
-CLASS_STEP = FRAMES * LIST_ROWS
+SEQS = SAMPLES * FRAMES
 TILES = [(kind, i) for i in range(FULL) for kind in range(KINDS)]
+EARLY_TILES = (0, 1, 2)
 LAST = KINDS * FULL
 
 FLOPS = 2 * SAMPLES * TOKENS * D * D
@@ -56,11 +57,6 @@ def transpose_pass(nc, banks, raw, ident, c):
     return bank
 
 
-def first_class(i):
-    sample = -(-i * P // CLASS_STEP)
-    return sample * CLASS_STEP - i * P, sample
-
-
 def tile_timesformerlayer_pc_kernel(tc, ctx_s, x_res, s_out_w, s_out_b, grad_out, out):
     nc = tc.nc
     with ExitStack() as ctx:
@@ -79,14 +75,10 @@ def tile_timesformerlayer_pc_kernel(tc, ctx_s, x_res, s_out_w, s_out_b, grad_out
         def load_g(pair):
             nc.sync.dma_start(out=g_raw[pair][:], in_=g_rows[pair])
 
-        load_w(0)
-        load_w(1)
-        load_g(0)
-        load_w(2)
-        load_w(3)
-        load_g(1)
-        load_g(2)
-        load_g(3)
+        for pair in range(W_PAIRS):
+            load_w(pair)
+        for pair in range(G_PAIRS):
+            load_g(pair)
 
         ident = keep.tile([P, P], F32, name="ident")
         make_identity(nc, ident[:])
@@ -104,25 +96,19 @@ def tile_timesformerlayer_pc_kernel(tc, ctx_s, x_res, s_out_w, s_out_b, grad_out
             nc.vector.memset(g_words[:, c, 0], 0.0)
         nc.vector.memset(g_words[:, :, 1, LIST:], 0.0)
 
-        is_class = keep.tile([P, FULL + 1], F32, name="is_class")
-        for i in range(FULL + 1):
-            columns = ident[:, first_class(i)[0] : P if i < FULL else REST : CLASS_STEP]
-            nc.vector.reduce_sum(out=is_class[:, i : i + 1], in_=columns, axis=mybir.AxisListType.X)
-        row_scale = keep.tile([P, FULL + 1], F32, name="row_scale")
-        nc.vector.tensor_scalar(
-            out=row_scale[:],
-            in0=is_class[:],
-            scalar1=1.0 / FRAMES - 1.0,
-            scalar2=1.0,
-            op0=mybir.AluOpType.mult,
-            op1=mybir.AluOpType.add,
+        spread = keep.tile([P, P], F32, name="spread")
+        nc.vector.memset(spread[:, SEQS:], 0.0)
+        nc.vector.tensor_copy(
+            out=spread[:, :SEQS].rearrange("k (b t) -> k b t", t=FRAMES),
+            in_=ident[:, REST : REST + SAMPLES].unsqueeze(2).to_broadcast([P, SAMPLES, FRAMES]),
         )
 
         def prepare_w(pair):
             rows = slice(pair * PAIR_ROWS, (pair + 1) * PAIR_ROWS)
             for c in range(PASSES):
                 bank = transpose_pass(nc, banks, w_raw[pair], ident, c)
-                nc.scalar.copy(out=w_words[:, c, rows, :], in_=bank[:].rearrange("q u i -> q i u"))
+                copy = nc.vector.tensor_copy if c == 0 and pair == W_PAIRS - 1 else nc.scalar.copy
+                copy(out=w_words[:, c, rows, :], in_=bank[:].rearrange("q u i -> q i u"))
 
         def quantise_w(pair):
             rows = slice(pair * PAIR_ROWS, (pair + 1) * PAIR_ROWS)
@@ -144,7 +130,10 @@ def tile_timesformerlayer_pc_kernel(tc, ctx_s, x_res, s_out_w, s_out_b, grad_out
                     g_words[:, c, kind, :LIST].rearrange("q (b t j) u -> q b t j u", t=FRAMES, j=LIST_ROWS)
                     for kind in range(KINDS)
                 ]
-                copy(out=even[:, samples, 0, 0, :], in_=tokens[:, :, :, 0].rearrange("q u b -> q b u"))
+                copy(
+                    out=g_words[:, c, 0, LIST + pair * PAIR_SAMPLES : LIST + (pair + 1) * PAIR_SAMPLES, :],
+                    in_=tokens[:, :, :, 0].rearrange("q u b -> q b u"),
+                )
                 copy(out=even[:, samples, :, 1:, :], in_=patches[:, :, :, 1::2, :].rearrange("q u b j t -> q b t j u"))
                 copy(out=odd[:, samples], in_=patches[:, :, :, 0::2, :].rearrange("q u b j t -> q b t j u"))
 
@@ -180,23 +169,11 @@ def tile_timesformerlayer_pc_kernel(tc, ctx_s, x_res, s_out_w, s_out_b, grad_out
             return acc
 
         def take_out(tile, half, acc):
-            target = h_rows[tile][:, half * N_HALF : (half + 1) * N_HALF]
-            if tile == LAST or TILES[tile][0] == 0:
-                i = FULL if tile == LAST else TILES[tile][1]
-                scale = row_scale[:, i : i + 1]
-                if half == 0:
-                    nc.scalar.activation(
-                        out=target, in_=acc[:], func=mybir.ActivationFunctionType.Copy, scale=scale
-                    )
-                else:
-                    nc.vector.tensor_scalar_mul(out=target, in0=acc[:], scalar1=scale)
-            elif half == 0:
-                nc.scalar.copy(out=target, in_=acc[:])
-            else:
-                nc.vector.tensor_copy(out=target, in_=acc[:])
+            copy = nc.scalar.copy if half == 0 or tile in EARLY_TILES else nc.vector.tensor_copy
+            copy(out=h_rows[tile][:, half * N_HALF : (half + 1) * N_HALF], in_=acc[:])
 
         list_rows = out.rearrange("s r d -> (s r) d").rearrange("(n kind) d -> kind n d", kind=KINDS)
-        class_rows = out.rearrange("(b t) r d -> b t r d", t=FRAMES)
+        class_rows = keep.tile([P, D], F32, name="class_rows")
 
         def store(tile):
             if tile < LAST:
@@ -209,16 +186,18 @@ def tile_timesformerlayer_pc_kernel(tc, ctx_s, x_res, s_out_w, s_out_b, grad_out
                     out=list_rows[kind, FULL * P : LIST, :], in_=h_rows[LAST][first : first + REST, :]
                 )
 
-        def copy_class_rows(i):
-            partition, sample = first_class(i)
-            stop = first_class(i + 1)[1] if i < FULL else SAMPLES
-            rows = h_rows[LAST if i == FULL else TILES.index((0, i))]
-            count = stop - sample
-            source = rows[partition : partition + (count - 1) * CLASS_STEP + 1 : CLASS_STEP, :]
-            nc.gpsimd.dma_start(
-                out=class_rows[sample:stop, 1:, 0, :],
-                in_=source.unsqueeze(1).to_broadcast([count, FRAMES - 1, D]),
-            )
+        def make_class_rows():
+            for half in range(HALVES):
+                cols = slice(half * N_HALF, (half + 1) * N_HALF)
+                acc = banks.tile([P, N_HALF], F32, name="class_acc", tag="bank")
+                nc.tensor.matmul(out=acc[:], lhsT=spread[:], rhs=h_rows[LAST][:, cols], start=True, stop=True)
+                if half == 0:
+                    nc.scalar.mul(out=class_rows[:, cols], in_=acc[:], mul=1.0 / FRAMES)
+                else:
+                    nc.vector.tensor_scalar_mul(out=class_rows[:, cols], in0=acc[:], scalar1=1.0 / FRAMES)
+
+        def store_class_rows():
+            nc.sync.dma_start(out=out[:, 0, :], in_=class_rows[:SEQS, :])
 
         def whole_tile(tile):
             for half in range(HALVES):
@@ -226,39 +205,31 @@ def tile_timesformerlayer_pc_kernel(tc, ctx_s, x_res, s_out_w, s_out_b, grad_out
             store(tile)
 
         prepare_w(0)
-        prepare_w(1)
-        quantise_w(0)
-        quantise_w(1)
+        for pair in range(1, W_PAIRS):
+            prepare_w(pair)
+            quantise_w(pair - 1)
         prepare_g(0)
         quantise_g(0)
-        quantise_g(1)
-        prepare_w(2)
-        for tile in (0, 1):
-            take_out(tile, 0, multiply(tile, 0))
-        prepare_w(3)
-        quantise_w(2)
         quantise_w(3)
+        quantise_g(1)
         prepare_g(1)
-        for tile in (0, 1):
-            take_out(tile, 1, multiply(tile, 1))
-            store(tile)
+        whole_tile(0)
         quantise_g(2)
         prepare_g(2)
-        whole_tile(2)
+        whole_tile(1)
         quantise_g(4)
-        copy_class_rows(0)
         prepare_g(3)
-        whole_tile(4)
-        copy_class_rows(1)
-        quantise_g(6)
+        whole_tile(2)
         quantise_g(LAST)
-        whole_tile(6)
-        copy_class_rows(2)
+        quantise_g(6)
+        whole_tile(4)
         quantise_g(3)
-        quantise_g(5)
         whole_tile(LAST)
-        copy_class_rows(3)
-        copy_class_rows(4)
+        quantise_g(5)
+        whole_tile(6)
+        make_class_rows()
         quantise_g(7)
-        for tile in (3, 5, 7):
-            whole_tile(tile)
+        whole_tile(3)
+        whole_tile(5)
+        store_class_rows()
+        whole_tile(7)

@@ -36,6 +36,7 @@ REST_COLS = P // KINDS
 LIST_COLS = FULL * P + REST_COLS
 SEQS = SAMPLES * FRAMES
 TILES = [(kind, i) for i in range(FULL) for kind in range(KINDS)]
+WARM_UPS = 4
 EARLY_TILES = (0, 1, 2)
 LAST = KINDS * FULL
 
@@ -83,6 +84,12 @@ def tile_timesformerlayer_pc_kernel(tc, ctx_s, x_res, s_out_w, s_out_b, grad_out
         ident = keep.tile([P, P], F32, name="ident")
         make_identity(nc, ident[:])
 
+        zeros = keep.tile([P, N_HALF], BF16, name="zeros")
+        nc.vector.memset(zeros[:], 0.0)
+        warm_bank = banks.tile([P, N_HALF], F32, name="warm_bank", tag="bank")
+        for i in range(WARM_UPS):
+            nc.tensor.matmul(out=warm_bank[:], lhsT=zeros[:, :P], rhs=zeros[:], start=True, stop=True)
+
         g_grouped = keep.tile([P, PASSES, KINDS, LIST_COLS * PACK], BF16, name="g_grouped", align_bytes=64)
         g_codes = keep.tile([P, LAST + 1, PASSES * P], U32, name="g_codes", align_bytes=64)
         g_scales = keep.tile([P, LAST + 1, PASSES * P], U8, name="g_scales", align_bytes=64)
@@ -96,12 +103,8 @@ def tile_timesformerlayer_pc_kernel(tc, ctx_s, x_res, s_out_w, s_out_b, grad_out
             nc.vector.memset(g_words[:, c, 0], 0.0)
         nc.vector.memset(g_words[:, :, 1, LIST:], 0.0)
 
-        spread = keep.tile([P, P], F32, name="spread")
-        nc.vector.memset(spread[:, SEQS:], 0.0)
-        nc.vector.tensor_copy(
-            out=spread[:, :SEQS].rearrange("k (b t) -> k b t", t=FRAMES),
-            in_=ident[:, REST : REST + SAMPLES].unsqueeze(2).to_broadcast([P, SAMPLES, FRAMES]),
-        )
+        turned = keep.tile([P, D // P, P], F32, name="turned")
+        nc.vector.memset(turned[:, :, SEQS:], 0.0)
 
         def prepare_w(pair):
             rows = slice(pair * PAIR_ROWS, (pair + 1) * PAIR_ROWS)
@@ -187,14 +190,31 @@ def tile_timesformerlayer_pc_kernel(tc, ctx_s, x_res, s_out_w, s_out_b, grad_out
                 )
 
         def make_class_rows():
+            blocks = N_HALF // P
+            for half in range(HALVES):
+                bank = banks.tile([P, blocks, P], F32, name="turned_bank", tag="bank")
+                for i in range(blocks):
+                    first = half * N_HALF + i * P
+                    nc.tensor.transpose(out=bank[:, i, :], in_=h_rows[LAST][:, first : first + P], identity=ident[:])
+                copy = nc.scalar.copy if half == 0 else nc.vector.tensor_copy
+                copy(
+                    out=turned[:, half * blocks : (half + 1) * blocks, :SEQS].rearrange("f i (b t) -> f i b t", t=FRAMES),
+                    in_=bank[:, :, REST : REST + SAMPLES].unsqueeze(3).to_broadcast([P, blocks, SAMPLES, FRAMES]),
+                )
+
+        def turn_class_rows_back():
+            blocks = N_HALF // P
             for half in range(HALVES):
                 cols = slice(half * N_HALF, (half + 1) * N_HALF)
-                acc = banks.tile([P, N_HALF], F32, name="class_acc", tag="bank")
-                nc.tensor.matmul(out=acc[:], lhsT=spread[:], rhs=h_rows[LAST][:, cols], start=True, stop=True)
+                bank = banks.tile([P, N_HALF], F32, name="class_bank", tag="bank")
+                for i in range(blocks):
+                    nc.tensor.transpose(
+                        out=bank[:, i * P : (i + 1) * P], in_=turned[:, half * blocks + i, :], identity=ident[:]
+                    )
                 if half == 0:
-                    nc.scalar.mul(out=class_rows[:, cols], in_=acc[:], mul=1.0 / FRAMES)
+                    nc.scalar.mul(out=class_rows[:, cols], in_=bank[:], mul=1.0 / FRAMES)
                 else:
-                    nc.vector.tensor_scalar_mul(out=class_rows[:, cols], in0=acc[:], scalar1=1.0 / FRAMES)
+                    nc.vector.tensor_scalar_mul(out=class_rows[:, cols], in0=bank[:], scalar1=1.0 / FRAMES)
 
         def store_class_rows():
             nc.sync.dma_start(out=out[:, 0, :], in_=class_rows[:SEQS, :])
@@ -203,6 +223,13 @@ def tile_timesformerlayer_pc_kernel(tc, ctx_s, x_res, s_out_w, s_out_b, grad_out
             for half in range(HALVES):
                 take_out(tile, half, multiply(tile, half))
             store(tile)
+
+        def final_tile(tile):
+            kind, i = TILES[tile]
+            for half in range(HALVES):
+                cols = slice(half * N_HALF, (half + 1) * N_HALF)
+                take_out(tile, half, multiply(tile, half))
+                nc.sync.dma_start(out=list_rows[kind, i * P : (i + 1) * P, cols], in_=h_rows[tile][:, cols])
 
         prepare_w(0)
         for pair in range(1, W_PAIRS):
@@ -230,6 +257,7 @@ def tile_timesformerlayer_pc_kernel(tc, ctx_s, x_res, s_out_w, s_out_b, grad_out
         make_class_rows()
         quantise_g(7)
         whole_tile(3)
+        turn_class_rows_back()
         whole_tile(5)
         store_class_rows()
-        whole_tile(7)
+        final_tile(7)

@@ -36,7 +36,7 @@ REST_COLS = P // KINDS
 LIST_COLS = FULL * P + REST_COLS
 SEQS = SAMPLES * FRAMES
 TILES = [(kind, i) for i in range(FULL) for kind in range(KINDS)]
-WARM_UPS = 4
+FIRST_WARM_UPS = 4
 EARLY_TILES = (0, 1, 2)
 LAST = KINDS * FULL
 
@@ -44,9 +44,13 @@ FLOPS = 2 * SAMPLES * TOKENS * D * D
 BYTES = 2 * (SAMPLES * TOKENS * D + D * D) + 4 * SAMPLES * FRAMES * (1 + PATCHES) * D
 
 
-def transpose_pass(nc, banks, raw, ident, c):
+def transpose_pass(nc, banks, raw, ident, c, zeros, warm_ups):
     words = raw[:].bitcast(F32)
     bank = banks.tile([P, PLANES, PAIR_ROWS], F32, name="bank", tag="bank")
+    for i in range(warm_ups):
+        nc.tensor.matmul(
+            out=bank[:].rearrange("q u i -> q (u i)"), lhsT=zeros[:, :P], rhs=zeros[:], start=True, stop=True
+        )
     for u in range(PLANES):
         first = (c * PLANES + u) * P
         for blk in range(PAIR_ROWS // P):
@@ -65,7 +69,7 @@ def tile_timesformerlayer_pc_kernel(tc, ctx_s, x_res, s_out_w, s_out_b, grad_out
         banks = ctx.enter_context(tc.psum_pool(name="banks", bufs=8))
         ctx.enter_context(tc.manual_schedule())
 
-        w_rows = s_out_w.rearrange("(pair blk p) k -> pair p blk k", blk=2, p=P)
+        w_rows = s_out_w.rearrange("(pair p r) k -> pair p r k", p=P, r=2)
         g_rows = grad_out.flatten_outer_dims().rearrange("(pair blk p) k -> pair p blk k", blk=2, p=P)
         w_raw = [keep.tile([P, 2, D], BF16, name="w_raw%d" % pair) for pair in range(W_PAIRS)]
         g_raw = [keep.tile([P, 2, D], BF16, name="g_raw%d" % pair) for pair in range(G_PAIRS)]
@@ -86,9 +90,6 @@ def tile_timesformerlayer_pc_kernel(tc, ctx_s, x_res, s_out_w, s_out_b, grad_out
 
         zeros = keep.tile([P, N_HALF], BF16, name="zeros")
         nc.vector.memset(zeros[:], 0.0)
-        warm_bank = banks.tile([P, N_HALF], F32, name="warm_bank", tag="bank")
-        for i in range(WARM_UPS):
-            nc.tensor.matmul(out=warm_bank[:], lhsT=zeros[:, :P], rhs=zeros[:], start=True, stop=True)
 
         g_grouped = keep.tile([P, PASSES, KINDS, LIST_COLS * PACK], BF16, name="g_grouped", align_bytes=64)
         g_codes = keep.tile([P, LAST + 1, PASSES * P], U32, name="g_codes", align_bytes=64)
@@ -109,9 +110,13 @@ def tile_timesformerlayer_pc_kernel(tc, ctx_s, x_res, s_out_w, s_out_b, grad_out
         def prepare_w(pair):
             rows = slice(pair * PAIR_ROWS, (pair + 1) * PAIR_ROWS)
             for c in range(PASSES):
-                bank = transpose_pass(nc, banks, w_raw[pair], ident, c)
+                warm_ups = 0 if c else FIRST_WARM_UPS if pair == 0 else 1
+                bank = transpose_pass(nc, banks, w_raw[pair], ident, c, zeros, warm_ups)
                 copy = nc.vector.tensor_copy if c == 0 and pair == W_PAIRS - 1 else nc.scalar.copy
-                copy(out=w_words[:, c, rows, :], in_=bank[:].rearrange("q u i -> q i u"))
+                copy(
+                    out=w_words[:, c, rows, :].rearrange("q (p r) u -> q p r u", r=2),
+                    in_=bank[:].rearrange("q u (r p) -> q p r u", r=2),
+                )
 
         def quantise_w(pair):
             rows = slice(pair * PAIR_ROWS, (pair + 1) * PAIR_ROWS)
@@ -125,7 +130,7 @@ def tile_timesformerlayer_pc_kernel(tc, ctx_s, x_res, s_out_w, s_out_b, grad_out
         def prepare_g(pair):
             samples = slice(pair * PAIR_SAMPLES, (pair + 1) * PAIR_SAMPLES)
             for c in range(PASSES):
-                bank = transpose_pass(nc, banks, g_raw[pair], ident, c)
+                bank = transpose_pass(nc, banks, g_raw[pair], ident, c, zeros, 1 if c == 0 and pair < 2 else 0)
                 tokens = bank[:].rearrange("q u (b n) -> q u b n", n=TOKENS)
                 patches = tokens[:, :, :, 1:].rearrange("q u b (p t) -> q u b p t", t=FRAMES)
                 copy = nc.vector.tensor_copy if c == 0 else nc.scalar.copy

from contextlib import ExitStack

import concourse.mybir as mybir
from concourse.masks import make_identity

F32 = mybir.dt.float32
BF16 = mybir.dt.bfloat16
U32 = mybir.dt.uint32
U8 = mybir.dt.uint8
E4M3_X4 = mybir.dt.float8_e4m3fn_x4
E5M2_X4 = mybir.dt.float8_e5m2_x4

P = 128
SAMPLES = 16
FRAMES = 7
PATCHES = 9
TOKENS = 64
D = 1024
PACK = 4
PASSES = D // (P * PACK)
PLANES = 2
N_HALF = 512
HALVES = D // N_HALF
PAIR_ROWS = 2 * P
PAIR_SAMPLES = PAIR_ROWS // TOKENS
W_PAIRS = D // PAIR_ROWS
G_PAIRS = SAMPLES * TOKENS // PAIR_ROWS

KINDS = 2
ROWS = 1 + PATCHES
LIST_ROWS = ROWS // KINDS
LIST = SAMPLES * FRAMES * LIST_ROWS
FULL = LIST // P
REST = LIST - FULL * P
REST_COLS = P // KINDS
LIST_COLS = FULL * P + REST_COLS
SEQS = SAMPLES * FRAMES
TILES = [(kind, i) for i in range(FULL) for kind in range(KINDS)]
FIRST_WARM_UPS = 4
EARLY_TILES = (0, 1, 2)
LAST = KINDS * FULL

FLOPS = 2 * SAMPLES * TOKENS * D * D
BYTES = 2 * (SAMPLES * TOKENS * D + D * D) + 4 * SAMPLES * FRAMES * (1 + PATCHES) * D


def transpose_pass(nc, banks, raw, ident, c, zeros, warm_ups):
    words = raw[:].bitcast(F32)
    bank = banks.tile([P, PLANES, PAIR_ROWS], F32, name="bank", tag="bank")
    for i in range(warm_ups):
        nc.tensor.matmul(
            out=bank[:].rearrange("q u i -> q (u i)"), lhsT=zeros[:, :P], rhs=zeros[:], start=True, stop=True
        )
    for u in range(PLANES):
        first = (c * PLANES + u) * P
        for blk in range(PAIR_ROWS // P):
            nc.tensor.transpose(
                out=bank[:, u, blk * P : (blk + 1) * P],
                in_=words[:, blk, first : first + P],
                identity=ident[:],
            )
    return bank


def tile_timesformerlayer_pc_kernel(tc, ctx_s, x_res, s_out_w, s_out_b, grad_out, out):
    nc = tc.nc
    with ExitStack() as ctx:
        keep = ctx.enter_context(tc.tile_pool(name="keep", bufs=1))
        banks = ctx.enter_context(tc.psum_pool(name="banks", bufs=8))
        ctx.enter_context(tc.manual_schedule())

        w_rows = s_out_w.rearrange("(pair p r) k -> pair p r k", p=P, r=2)
        g_rows = grad_out.flatten_outer_dims().rearrange("(pair blk p) k -> pair p blk k", blk=2, p=P)
        w_raw = [keep.tile([P, 2, D], BF16, name="w_raw%d" % pair) for pair in range(W_PAIRS)]
        g_raw = [keep.tile([P, 2, D], BF16, name="g_raw%d" % pair) for pair in range(G_PAIRS)]

        def load_w(pair):
            nc.sync.dma_start(out=w_raw[pair][:], in_=w_rows[pair])

        def load_g(pair):
            nc.sync.dma_start(out=g_raw[pair][:], in_=g_rows[pair])

        for pair in range(W_PAIRS):
            load_w(pair)
        for pair in range(G_PAIRS):
            load_g(pair)

        ident = keep.tile([P, P], F32, name="ident")
        make_identity(nc, ident[:])

        zeros = keep.tile([P, N_HALF], BF16, name="zeros")
        nc.vector.memset(zeros[:], 0.0)

        g_grouped = keep.tile([P, PASSES, KINDS, LIST_COLS * PACK], BF16, name="g_grouped", align_bytes=64)
        g_codes = keep.tile([P, LAST + 1, PASSES * P], U32, name="g_codes", align_bytes=64)
        g_scales = keep.tile([P, LAST + 1, PASSES * P], U8, name="g_scales", align_bytes=64)
        g_words = g_grouped[:].bitcast(F32).rearrange("q c l (m u) -> q c l m u", u=PLANES)
        w_grouped = keep.tile([P, PASSES, D * PACK], BF16, name="w_grouped", align_bytes=64)
        w_codes = keep.tile([P, PASSES, D], U32, name="w_codes", align_bytes=64)
        w_scales = keep.tile([P, PASSES, D], U8, name="w_scales", align_bytes=64)
        w_words = w_grouped[:].bitcast(F32).rearrange("q c (i u) -> q c i u", u=PLANES)

        for c in range(PASSES):
            nc.vector.memset(g_words[:, c, 0], 0.0)
        nc.vector.memset(g_words[:, :, 1, LIST:], 0.0)

        turned = keep.tile([P, D // P, P], F32, name="turned")
        nc.vector.memset(turned[:, :, SEQS:], 0.0)

        def prepare_w(pair):
            rows = slice(pair * PAIR_ROWS, (pair + 1) * PAIR_ROWS)
            for c in range(PASSES):
                warm_ups = 0 if c else FIRST_WARM_UPS if pair == 0 else 1
                bank = transpose_pass(nc, banks, w_raw[pair], ident, c, zeros, warm_ups)
                copy = nc.vector.tensor_copy if c == 0 and pair == W_PAIRS - 1 else nc.scalar.copy
                copy(
                    out=w_words[:, c, rows, :].rearrange("q (p r) u -> q p r u", r=2),
                    in_=bank[:].rearrange("q u (r p) -> q p r u", r=2),
                )

        def quantise_w(pair):
            rows = slice(pair * PAIR_ROWS, (pair + 1) * PAIR_ROWS)
            for c in range(PASSES):
                nc.vector.quantize_mx(
                    out=w_codes[:, c, rows].bitcast(E4M3_X4),
                    scales=w_scales[:, c, rows],
                    in_=w_grouped[:, c, pair * PAIR_ROWS * PACK : (pair + 1) * PAIR_ROWS * PACK],
                )

        def prepare_g(pair):
            samples = slice(pair * PAIR_SAMPLES, (pair + 1) * PAIR_SAMPLES)
            for c in range(PASSES):
                bank = transpose_pass(nc, banks, g_raw[pair], ident, c, zeros, 1 if c == 0 and pair < 2 else 0)
                tokens = bank[:].rearrange("q u (b n) -> q u b n", n=TOKENS)
                patches = tokens[:, :, :, 1:].rearrange("q u b (p t) -> q u b p t", t=FRAMES)
                copy = nc.vector.tensor_copy if c == 0 else nc.scalar.copy
                even, odd = [
                    g_words[:, c, kind, :LIST].rearrange("q (b t j) u -> q b t j u", t=FRAMES, j=LIST_ROWS)
                    for kind in range(KINDS)
                ]
                copy(
                    out=g_words[:, c, 0, LIST + pair * PAIR_SAMPLES : LIST + (pair + 1) * PAIR_SAMPLES, :],
                    in_=tokens[:, :, :, 0].rearrange("q u b -> q b u"),
                )
                copy(out=even[:, samples, :, 1:, :], in_=patches[:, :, :, 1::2, :].rearrange("q u b j t -> q b t j u"))
                copy(out=odd[:, samples], in_=patches[:, :, :, 0::2, :].rearrange("q u b j t -> q b t j u"))

        def quantise_g(tile):
            for c in range(PASSES):
                if tile < LAST:
                    pieces = [(TILES[tile][0], TILES[tile][1] * P, P, 0)]
                else:
                    pieces = [(kind, FULL * P, REST_COLS, kind * REST_COLS) for kind in range(KINDS)]
                for kind, source, width, offset in pieces:
                    columns = slice(c * P + offset, c * P + offset + width)
                    nc.vector.quantize_mx(
                        out=g_codes[:, tile, columns].bitcast(E5M2_X4),
                        scales=g_scales[:, tile, columns],
                        in_=g_grouped[:, c, kind, source * PACK : (source + width) * PACK],
                    )

        h_rows = [keep.tile([P, D], F32, name="h_rows%d" % tile) for tile in range(LAST + 1)]

        def multiply(tile, half):
            cols = slice(half * N_HALF, (half + 1) * N_HALF)
            acc = banks.tile([P, N_HALF], F32, name="acc", tag="bank")
            for c in range(PASSES):
                nc.tensor.matmul_mx(
                    out=acc[:],
                    lhsT=g_codes[:, tile, c * P : (c + 1) * P].bitcast(E5M2_X4),
                    lhsT_scale=g_scales[:, tile, c * P : (c + 1) * P],
                    rhs=w_codes[:, c, cols].bitcast(E4M3_X4),
                    rhs_scale=w_scales[:, c, cols],
                    start=(c == 0),
                    stop=(c == PASSES - 1),
                )
            return acc

        def take_out(tile, half, acc):
            copy = nc.scalar.copy if half == 0 or tile in EARLY_TILES else nc.vector.tensor_copy
            copy(out=h_rows[tile][:, half * N_HALF : (half + 1) * N_HALF], in_=acc[:])

        list_rows = out.rearrange("s r d -> (s r) d").rearrange("(n kind) d -> kind n d", kind=KINDS)
        class_rows = keep.tile([P, D], F32, name="class_rows")

        def store(tile):
            if tile < LAST:
                kind, i = TILES[tile]
                nc.sync.dma_start(out=list_rows[kind, i * P : (i + 1) * P, :], in_=h_rows[tile][:])
                return
            for kind in range(KINDS):
                first = kind * REST_COLS
                nc.sync.dma_start(
                    out=list_rows[kind, FULL * P : LIST, :], in_=h_rows[LAST][first : first + REST, :]
                )

        def make_class_rows():
            blocks = N_HALF // P
            for half in range(HALVES):
                bank = banks.tile([P, blocks, P], F32, name="turned_bank", tag="bank")
                for i in range(blocks):
                    first = half * N_HALF + i * P
                    nc.tensor.transpose(out=bank[:, i, :], in_=h_rows[LAST][:, first : first + P], identity=ident[:])
                copy = nc.scalar.copy if half == 0 else nc.vector.tensor_copy
                copy(
                    out=turned[:, half * blocks : (half + 1) * blocks, :SEQS].rearrange("f i (b t) -> f i b t", t=FRAMES),
                    in_=bank[:, :, REST : REST + SAMPLES].unsqueeze(3).to_broadcast([P, blocks, SAMPLES, FRAMES]),
                )

        def turn_class_rows_back():
            blocks = N_HALF // P
            for half in range(HALVES):
                cols = slice(half * N_HALF, (half + 1) * N_HALF)
                bank = banks.tile([P, N_HALF], F32, name="class_bank", tag="bank")
                for i in range(blocks):
                    nc.tensor.transpose(
                        out=bank[:, i * P : (i + 1) * P], in_=turned[:, half * blocks + i, :], identity=ident[:]
                    )
                if half == 0:
                    nc.scalar.mul(out=class_rows[:, cols], in_=bank[:], mul=1.0 / FRAMES)
                else:
                    nc.vector.tensor_scalar_mul(out=class_rows[:, cols], in0=bank[:], scalar1=1.0 / FRAMES)

        def store_class_rows():
            nc.sync.dma_start(out=out[:, 0, :], in_=class_rows[:SEQS, :])

        def whole_tile(tile):
            for half in range(HALVES):
                take_out(tile, half, multiply(tile, half))
            store(tile)

        def final_tile(tile):
            kind, i = TILES[tile]
            for half in range(HALVES):
                cols = slice(half * N_HALF, (half + 1) * N_HALF)
                take_out(tile, half, multiply(tile, half))
                nc.sync.dma_start(out=list_rows[kind, i * P : (i + 1) * P, cols], in_=h_rows[tile][:, cols])

        prepare_w(0)
        for pair in range(1, W_PAIRS):
            prepare_w(pair)
            quantise_w(pair - 1)
        prepare_g(0)
        quantise_g(0)
        quantise_w(3)
        quantise_g(1)
        prepare_g(1)
        whole_tile(0)
        quantise_g(2)
        prepare_g(2)
        whole_tile(1)
        quantise_g(4)
        prepare_g(3)
        whole_tile(2)
        quantise_g(LAST)
        quantise_g(6)
        whole_tile(4)
        quantise_g(3)
        whole_tile(LAST)
        quantise_g(5)
        whole_tile(6)
        make_class_rows()
        quantise_g(7)
        whole_tile(3)
        turn_class_rows_back()
        whole_tile(5)
        store_class_rows()
        final_tile(7)
